import numpy as np
import ml_dtypes


def mxq(x, axis, fmt="e4m3"):
    dtype, down = {"e4m3": (ml_dtypes.float8_e4m3fn, 7), "e5m2": (ml_dtypes.float8_e5m2, 14)}[fmt]
    v = np.moveaxis(np.asarray(x, np.float32).astype(ml_dtypes.bfloat16).astype(np.float64), axis, -1)
    blocks = v.reshape(v.shape[:-1] + (-1, 32))
    amax = np.abs(blocks).max(-1, keepdims=True)
    byte = np.maximum(np.where(amax > 0, np.frexp(amax)[1] - 1 + 127, 0) - down, 1)
    scale = np.exp2(byte - 127.0)
    codes = (blocks / scale).astype(np.float32).astype(dtype).astype(np.float64)
    return np.moveaxis((codes * scale).reshape(v.shape), -1, axis)


WIDE = False


def mx_kscale(k):
    if not WIDE:
        return np.ones(k)
    levels = np.array([10, -10, 5, -5, 0])
    if k % 512:
        return np.exp2(np.random.permutation(np.resize(levels, k // 32))).repeat(32)
    a = np.empty((k // 512, 16))
    for p in range(k // 512):
        a[p, :8] = np.random.permutation(np.resize(levels, 8))
        for g in range(8):
            far = levels[np.abs(levels - a[p, g]) >= 10]
            a[p, g + 8] = far[np.random.randint(len(far))]
    return np.exp2(a.ravel()).repeat(32)


BF16 = ml_dtypes.bfloat16


def bf(x):
    return np.asarray(x, np.float32).astype(BF16)


def f64(x):
    return np.asarray(x).astype(np.float64)


B, N, I, O = 4096, 5, 512, 128
WS = 0.7 / np.sqrt(I)


def setup_inputs():
    s = mx_kscale(I)
    return {"x": bf((np.random.standard_normal((B, N, I)) * s).reshape(B, N * I)),
            "w_self": bf(np.random.standard_normal((N, O, I)) * WS / s),
            "w_parent": bf(np.random.standard_normal((N - 1, O, I)) * WS / s),
            "bias": bf(np.random.standard_normal(N * O) * 0.5)}


def reference(x, w_self, w_parent, bias):
    xq = mxq(f64(x).reshape(B, N, I).transpose(1, 0, 2), 2, "e4m3")
    y_self = xq @ mxq(f64(w_self).transpose(0, 2, 1), 1, "e4m3")
    y_par = xq[:-1] @ mxq(f64(w_parent).transpose(0, 2, 1), 1, "e4m3")
    y = np.concatenate([y_self[:1], y_self[1:] + y_par], 0)
    return y.transpose(1, 0, 2).reshape(B, N * O) + f64(bias)

@@ -1,0 +1,198 @@
+from contextlib import ExitStack
+
+import concourse.mybir as mybir
+from concourse.masks import make_identity
+
+F32 = mybir.dt.float32
+BF16 = mybir.dt.bfloat16
+U32 = mybir.dt.uint32
+U8 = mybir.dt.uint8
+FP8X4 = mybir.dt.float8_e4m3fn_x4
+ADD = mybir.AluOpType.add
+
+P = 128
+B, N, I, O = 4096, 5, 512, 128
+FLOPS = 2 * B * I * O * (2 * N - 1)
+
+CHUNKS = [4, 4, 4, 4, 4, 4, 4, 2, 2]
+XBUFS = 4
+OBUFS = 5
+LEAD = 3
+
+
+def tile_skeletonlinear_pa_t_kernel(tc, x, w_self, w_parent, bias, out):
+    nc = tc.nc
+    assert sum(CHUNKS) * P == B
+
+    chunk_base = []
+    tiles = []
+    for c, T in enumerate(CHUNKS):
+        chunk_base.append(P * len(tiles))
+        for t in range(T):
+            tiles.append((c, t))
+    n_tiles = len(tiles)
+
+    with ExitStack() as ctx:
+        const = ctx.enter_context(tc.tile_pool(name="const", bufs=1))
+        xpool = ctx.enter_context(tc.tile_pool(name="xin", bufs=XBUFS))
+        gpool = ctx.enter_context(tc.tile_pool(name="grp", bufs=3))
+        qpool = ctx.enter_context(tc.tile_pool(name="qnt", bufs=4))
+        opool = ctx.enter_context(tc.tile_pool(name="res", bufs=OBUFS))
+        pst = ctx.enter_context(tc.psum_pool(name="pst", bufs=4))
+        pso = ctx.enter_context(tc.psum_pool(name="pso", bufs=2))
+        psc = ctx.enter_context(tc.psum_pool(name="psc", bufs=2))
+        ctx.enter_context(tc.manual_schedule())
+
+        x_tiles = {}
+
+        def load(c):
+            T = CHUNKS[c]
+            xt = xpool.tile([P, T * N * I], BF16, name="xt", tag="xt")
+            r0 = chunk_base[c]
+            nc.sync.dma_start(
+                out=xt[:], in_=x[r0 : r0 + P * T, :].rearrange("(p t) c -> p (t c)", t=T)
+            )
+            x_tiles[c] = xt
+
+        ident = const.tile([P, P], F32, name="ident")
+        make_identity(nc, ident[:])
+        ones = const.tile([P, P], BF16, name="ones")
+        nc.vector.memset(ones[:], 1.0)
+        brow = const.tile([P, 768], BF16, name="brow")
+        nc.vector.memset(brow[:], 0.0)
+        nc.sync.dma_start(out=brow[0:1, 0 : N * O], in_=bias.unsqueeze(0))
+        wsb = const.tile([P, 9 * I], BF16, name="wsb")
+        nc.sync.dma_start(
+            out=wsb[:, 0 : 5 * I].rearrange("o (n i) -> o n i", n=5),
+            in_=w_self.rearrange("n o i -> o n i"),
+        )
+        nc.sync.dma_start(
+            out=wsb[:, 5 * I : 9 * I].rearrange("o (n i) -> o n i", n=4),
+            in_=w_parent.rearrange("n o i -> o n i"),
+        )
+        for c in range(min(XBUFS, len(CHUNKS))):
+            load(c)
+
+        def flip(src32, cols, dst32):
+            n = len(cols)
+            tp = pst.tile([P, 2, 256], F32, name="tp", tag="tp")
+            for u in range(2):
+                for q in range(n):
+                    c0 = cols[q]
+                    nc.tensor.transpose(
+                        tp[:, u, q * P : (q + 1) * P], src32[:, c0 + u : c0 + 2 * P : 2], ident[:]
+                    )
+            nc.scalar.copy(
+                out=dst32.rearrange("p (c u) -> p c u", u=2),
+                in_=tp[:, :, 0 : n * P].rearrange("p u c -> p c u"),
+            )
+
+        ww = wsb[:].bitcast(F32)
+        wg = gpool.tile([P, N * 1024], BF16, name="wg", tag="g", align_bytes=64)
+        wg32 = wg[:].bitcast(F32)
+        for i in range(5):
+            blocks = [b for b in (2 * i, 2 * i + 1) if b < 9]
+            flip(ww, [b * 256 for b in blocks], wg32[:, i * 512 : i * 512 + len(blocks) * 256])
+        wq = const.tile([P, 9 * O], U32, name="wq", align_bytes=64)
+        wsc = const.tile([P, 9 * O], U8, name="wsc", align_bytes=64)
+        nc.vector.quantize_mx(out=wq[:, 0:1024].bitcast(FP8X4), scales=wsc[:, 0:1024], in_=wg[:, 0:4096])
+        nc.vector.quantize_mx(
+            out=wq[:, 1024:1152].bitcast(FP8X4), scales=wsc[:, 1024:1152], in_=wg[:, 4096:4608]
+        )
+
+        bp0 = pso.tile([P, 512], F32, name="bp0", tag="o")
+        nc.tensor.matmul(bp0[:], lhsT=ones[:], rhs=brow[:, 0:512], start=True, stop=True)
+        bp1 = pso.tile([P, 512], F32, name="bp1", tag="o")
+        nc.tensor.matmul(bp1[:, 0:256], lhsT=ones[:], rhs=brow[:, 512:768], start=True, stop=True)
+        bias_a = const.tile([P, 512], F32, name="bias_a")
+        nc.vector.tensor_copy(out=bias_a[:], in_=bp0[:])
+        bias_c = const.tile([P, 512], F32, name="bias_c")
+        for t in range(4):
+            nc.vector.tensor_copy(out=bias_c[:, t * O : (t + 1) * O], in_=bp1[:, 0:O])
+
+        g_tiles = {}
+        q_tiles = {}
+        c_tiles = {}
+        o_tiles = {}
+
+        def transposes(h):
+            k, part = divmod(h, 2)
+            c, t0 = tiles[2 * k]
+            xw = x_tiles[c][:].bitcast(F32)
+            if part == 0:
+                g_tiles[k] = gpool.tile([P, N * 1024], BF16, name="g", tag="g", align_bytes=64)
+            g32 = g_tiles[k][:].bitcast(F32)
+            for j in ((0, 1) if part == 0 else (2, 3, 4)):
+                flip(
+                    xw,
+                    [(t0 + q) * (N * 256) + j * 256 for q in range(2)],
+                    g32[:, j * 512 : (j + 1) * 512],
+                )
+            if part == 1 and t0 + 2 == CHUNKS[c] and c + XBUFS < len(CHUNKS):
+                load(c + XBUFS)
+
+        def quantise(h):
+            k, part = divmod(h, 2)
+            g = g_tiles[k]
+            if part == 0:
+                xq = qpool.tile([P, N * 256], U32, name="xq", tag="xq", align_bytes=64)
+                xs = qpool.tile([P, N * 256], U8, name="xs", tag="xs", align_bytes=64)
+                q_tiles[k] = (xq, xs)
+                spans = [(0, 512)]
+            else:
+                xq, xs = q_tiles[k]
+                spans = [(512, 1024), (1024, 1280)]
+            for a, b in spans:
+                nc.vector.quantize_mx(
+                    out=xq[:, a:b].bitcast(FP8X4), scales=xs[:, a:b], in_=g[:, 4 * a : 4 * b]
+                )
+
+        def mx(acc, xq, xs, col, b, start, stop):
+            nc.tensor.matmul_mx(
+                out=acc,
+                lhsT=xq[:, col : col + P].bitcast(FP8X4),
+                lhsT_scale=xs[:, col : col + P],
+                rhs=wq[:, b * O : (b + 1) * O].bitcast(FP8X4),
+                rhs_scale=wsc[:, b * O : (b + 1) * O],
+                start=start,
+                stop=stop,
+            )
+
+        def passes(s):
+            c, t = tiles[s]
+            T = CHUNKS[c]
+            xq, xs = q_tiles[s // 2]
+            q = s % 2
+            acc = pso.tile([P, 512], F32, name="acc", tag="o")
+            if t == 0:
+                c_tiles[c] = psc.tile([P, 512], F32, name="acc4", tag="c")
+                o_tiles[c] = opool.tile([P, T * N * O], F32, name="res", tag="res")
+            acc4 = c_tiles[c]
+            res = o_tiles[c]
+            for j in range(N):
+                dst = acc[:, j * O : (j + 1) * O] if j < 4 else acc4[:, t * O : (t + 1) * O]
+                if j > 0:
+                    mx(dst, xq, xs, (j - 1) * 256 + q * P, 5 + j - 1, True, False)
+                mx(dst, xq, xs, j * 256 + q * P, j, j == 0, True)
+            nc.vector.tensor_tensor(
+                out=res[:, t * N * O : t * N * O + 512], in0=acc[:], in1=bias_a[:], op=ADD
+            )
+            if t == T - 1:
+                nc.vector.tensor_tensor(
+                    out=res[:].rearrange("p (t c) -> p t c", t=T)[:, :, 512:640],
+                    in0=acc4[:, 0 : T * O].rearrange("p (t c) -> p t c", t=T),
+                    in1=bias_c[:, 0 : T * O].rearrange("p (t c) -> p t c", t=T),
+                    op=ADD,
+                )
+                r0 = chunk_base[c]
+                nc.sync.dma_start(
+                    out=out[r0 : r0 + P * T, :].rearrange("(p t) c -> p (t c)", t=T), in_=res[:]
+                )
+
+        for s in range(-LEAD, n_tiles):
+            if s + LEAD < n_tiles:
+                transposes(s + LEAD)
+            if 0 <= s + LEAD - 1 < n_tiles:
+                quantise(s + LEAD - 1)
+            if s >= 0:
+                passes(s)

@@ -15,9 +15,11 @@ B, N, I, O = 4096, 5, 512, 128
 FLOPS = 2 * B * I * O * (2 * N - 1)
 
 CHUNKS = [4, 4, 4, 4, 4, 4, 4, 2, 2]
-XBUFS = 4
-OBUFS = 5
+XBUFS = 9
+OBUFS = 4
 LEAD = 3
+VJ = 2
+SJ = 3
 
 
 def tile_skeletonlinear_pa_t_kernel(tc, x, w_self, w_parent, bias, out):
@@ -37,6 +39,7 @@ def tile_skeletonlinear_pa_t_kernel(tc, x, w_self, w_parent, bias, out):
         xpool = ctx.enter_context(tc.tile_pool(name="xin", bufs=XBUFS))
         gpool = ctx.enter_context(tc.tile_pool(name="grp", bufs=3))
         qpool = ctx.enter_context(tc.tile_pool(name="qnt", bufs=4))
+        spool = ctx.enter_context(tc.tile_pool(name="spl", bufs=2))
         opool = ctx.enter_context(tc.tile_pool(name="res", bufs=OBUFS))
         pst = ctx.enter_context(tc.psum_pool(name="pst", bufs=4))
         pso = ctx.enter_context(tc.psum_pool(name="pso", bufs=2))
@@ -45,43 +48,43 @@ def tile_skeletonlinear_pa_t_kernel(tc, x, w_self, w_parent, bias, out):
 
         x_tiles = {}
 
-        def load(c):
+        def load(k):
+            c, t0 = tiles[2 * k]
             T = CHUNKS[c]
-            xt = xpool.tile([P, T * N * I], BF16, name="xt", tag="xt")
+            xt = xpool.tile([P, 2 * N * I], BF16, name="xt", tag="xt")
             r0 = chunk_base[c]
+            rows = x[r0 : r0 + P * T, :].rearrange("(p t) c -> p t c", t=T)
             nc.sync.dma_start(
-                out=xt[:], in_=x[r0 : r0 + P * T, :].rearrange("(p t) c -> p (t c)", t=T)
+                out=xt[:].rearrange("p (t c) -> p t c", t=2), in_=rows[:, t0 : t0 + 2, :]
             )
-            x_tiles[c] = xt
+            x_tiles[k] = xt
 
         ident = const.tile([P, P], F32, name="ident")
         make_identity(nc, ident[:])
         ones = const.tile([P, P], BF16, name="ones")
-        nc.vector.memset(ones[:], 1.0)
+        nc.gpsimd.memset(ones[:], 1.0)
         brow = const.tile([P, 768], BF16, name="brow")
-        nc.vector.memset(brow[:], 0.0)
-        nc.sync.dma_start(out=brow[0:1, 0 : N * O], in_=bias.unsqueeze(0))
+        nc.gpsimd.memset(brow[:], 0.0)
         wsb = const.tile([P, 9 * I], BF16, name="wsb")
         nc.sync.dma_start(
             out=wsb[:, 0 : 5 * I].rearrange("o (n i) -> o n i", n=5),
             in_=w_self.rearrange("n o i -> o n i"),
         )
+        load(0)
         nc.sync.dma_start(
             out=wsb[:, 5 * I : 9 * I].rearrange("o (n i) -> o n i", n=4),
             in_=w_parent.rearrange("n o i -> o n i"),
         )
-        for c in range(min(XBUFS, len(CHUNKS))):
-            load(c)
+        nc.sync.dma_start(out=brow[0:1, 0 : N * O], in_=bias.unsqueeze(0))
+        for k in range(1, XBUFS):
+            load(k)
 
-        def flip(src32, cols, dst32):
-            n = len(cols)
+        def flip(blocks, dst32):
+            n = len(blocks)
             tp = pst.tile([P, 2, 256], F32, name="tp", tag="tp")
             for u in range(2):
                 for q in range(n):
-                    c0 = cols[q]
-                    nc.tensor.transpose(
-                        tp[:, u, q * P : (q + 1) * P], src32[:, c0 + u : c0 + 2 * P : 2], ident[:]
-                    )
+                    nc.tensor.transpose(tp[:, u, q * P : (q + 1) * P], blocks[q][u], ident[:])
             nc.scalar.copy(
                 out=dst32.rearrange("p (c u) -> p c u", u=2),
                 in_=tp[:, :, 0 : n * P].rearrange("p u c -> p c u"),
@@ -90,46 +93,74 @@ def tile_skeletonlinear_pa_t_kernel(tc, x, w_self, w_parent, bias, out):
         ww = wsb[:].bitcast(F32)
         wg = gpool.tile([P, N * 1024], BF16, name="wg", tag="g", align_bytes=64)
         wg32 = wg[:].bitcast(F32)
-        for i in range(5):
-            blocks = [b for b in (2 * i, 2 * i + 1) if b < 9]
-            flip(ww, [b * 256 for b in blocks], wg32[:, i * 512 : i * 512 + len(blocks) * 256])
         wq = const.tile([P, 9 * O], U32, name="wq", align_bytes=64)
         wsc = const.tile([P, 9 * O], U8, name="wsc", align_bytes=64)
-        nc.vector.quantize_mx(out=wq[:, 0:1024].bitcast(FP8X4), scales=wsc[:, 0:1024], in_=wg[:, 0:4096])
-        nc.vector.quantize_mx(
-            out=wq[:, 1024:1152].bitcast(FP8X4), scales=wsc[:, 1024:1152], in_=wg[:, 4096:4608]
-        )
 
-        bp0 = pso.tile([P, 512], F32, name="bp0", tag="o")
-        nc.tensor.matmul(bp0[:], lhsT=ones[:], rhs=brow[:, 0:512], start=True, stop=True)
-        bp1 = pso.tile([P, 512], F32, name="bp1", tag="o")
-        nc.tensor.matmul(bp1[:, 0:256], lhsT=ones[:], rhs=brow[:, 512:768], start=True, stop=True)
+        def weights(first, count):
+            for b0 in range(first, first + count, 2):
+                pair = range(b0, min(b0 + 2, first + count))
+                blocks = [[ww[:, b * 256 + u : (b + 1) * 256 : 2] for u in range(2)] for b in pair]
+                flip(blocks, wg32[:, b0 * 256 : (b0 + len(pair)) * 256])
+            for b0, n in ((first, 4), (first + 4, count - 4)):
+                if n:
+                    cols = slice(b0 * O, (b0 + n) * O)
+                    nc.vector.quantize_mx(
+                        out=wq[:, cols].bitcast(FP8X4), scales=wsc[:, cols], in_=wg[:, b0 * I : (b0 + n) * I]
+                    )
+
         bias_a = const.tile([P, 512], F32, name="bias_a")
-        nc.vector.tensor_copy(out=bias_a[:], in_=bp0[:])
         bias_c = const.tile([P, 512], F32, name="bias_c")
-        for t in range(4):
-            nc.vector.tensor_copy(out=bias_c[:, t * O : (t + 1) * O], in_=bp1[:, 0:O])
+
+        def spread_bias():
+            bp0 = pso.tile([P, 512], F32, name="bp0", tag="o")
+            nc.tensor.matmul(bp0[:], lhsT=ones[:], rhs=brow[:, 0:512], start=True, stop=True)
+            bp1 = pso.tile([P, 512], F32, name="bp1", tag="o")
+            nc.tensor.matmul(bp1[:, 0:256], lhsT=ones[:], rhs=brow[:, 512:768], start=True, stop=True)
+            nc.scalar.copy(out=bias_a[:], in_=bp0[:])
+            for t in range(4):
+                nc.scalar.copy(out=bias_c[:, t * O : (t + 1) * O], in_=bp1[:, 0:O])
 
         g_tiles = {}
         q_tiles = {}
         c_tiles = {}
         o_tiles = {}
 
+        s_tiles = {}
+
+        def split(k):
+            xw = x_tiles[k][:].bitcast(F32).rearrange("p (t w) -> p t w", t=2)
+            sv = spool.tile([P, 2, 2, VJ * P], F32, name="sv", tag="sv")
+            nc.vector.tensor_copy(
+                out=sv[:], in_=xw[:, :, 0 : VJ * 256].rearrange("p t (w u) -> p t u w", u=2)
+            )
+            ss = spool.tile([P, 2, 2, (SJ - VJ) * P], F32, name="ss", tag="ss")
+            nc.scalar.copy(
+                out=ss[:], in_=xw[:, :, VJ * 256 : SJ * 256].rearrange("p t (w u) -> p t u w", u=2)
+            )
+            s_tiles[k] = (sv, ss)
+
+        def block(k, xw, j, q, u):
+            sv, ss = s_tiles[k]
+            if j < VJ:
+                return sv[:, q, u, j * P : (j + 1) * P]
+            if j < SJ:
+                return ss[:, q, u, (j - VJ) * P : (j - VJ + 1) * P]
+            c0 = q * (N * 256) + j * 256
+            return xw[:, c0 + u : c0 + 256 : 2]
+
         def transposes(h):
             k, part = divmod(h, 2)
-            c, t0 = tiles[2 * k]
-            xw = x_tiles[c][:].bitcast(F32)
+            xw = x_tiles[k][:].bitcast(F32)
             if part == 0:
                 g_tiles[k] = gpool.tile([P, N * 1024], BF16, name="g", tag="g", align_bytes=64)
             g32 = g_tiles[k][:].bitcast(F32)
             for j in ((0, 1) if part == 0 else (2, 3, 4)):
                 flip(
-                    xw,
-                    [(t0 + q) * (N * 256) + j * 256 for q in range(2)],
+                    [[block(k, xw, j, q, u) for u in range(2)] for q in range(2)],
                     g32[:, j * 512 : (j + 1) * 512],
                 )
-            if part == 1 and t0 + 2 == CHUNKS[c] and c + XBUFS < len(CHUNKS):
-                load(c + XBUFS)
+            if part == 1 and k + XBUFS < n_tiles // 2:
+                load(k + XBUFS)
 
         def quantise(h):
             k, part = divmod(h, 2)
@@ -189,7 +220,13 @@ def tile_skeletonlinear_pa_t_kernel(tc, x, w_self, w_parent, bias, out):
                     out=out[r0 : r0 + P * T, :].rearrange("(p t) c -> p (t c)", t=T), in_=res[:]
                 )
 
+        weights(0, 5)
+        split(0)
+        weights(5, 4)
+        spread_bias()
         for s in range(-LEAD, n_tiles):
+            if s + LEAD + 2 < n_tiles and (s + LEAD) % 2 == 0:
+                split((s + LEAD + 2) // 2)
             if s + LEAD < n_tiles:
                 transposes(s + LEAD)
             if 0 <= s + LEAD - 1 < n_tiles:

@@ -19,7 +19,6 @@ XBUFS = 9
 OBUFS = 4
 LEAD = 3
 VJ = 2
-SJ = 3
 
 
 def tile_skeletonlinear_pa_t_kernel(tc, x, w_self, w_parent, bias, out):
@@ -108,17 +107,15 @@ def tile_skeletonlinear_pa_t_kernel(tc, x, w_self, w_parent, bias, out):
                         out=wq[:, cols].bitcast(FP8X4), scales=wsc[:, cols], in_=wg[:, b0 * I : (b0 + n) * I]
                     )
 
-        bias_a = const.tile([P, 512], F32, name="bias_a")
-        bias_c = const.tile([P, 512], F32, name="bias_c")
+        bias_t = const.tile([P, N * O], F32, name="bias_t")
 
         def spread_bias():
             bp0 = pso.tile([P, 512], F32, name="bp0", tag="o")
             nc.tensor.matmul(bp0[:], lhsT=ones[:], rhs=brow[:, 0:512], start=True, stop=True)
             bp1 = pso.tile([P, 512], F32, name="bp1", tag="o")
             nc.tensor.matmul(bp1[:, 0:256], lhsT=ones[:], rhs=brow[:, 512:768], start=True, stop=True)
-            nc.scalar.copy(out=bias_a[:], in_=bp0[:])
-            for t in range(4):
-                nc.scalar.copy(out=bias_c[:, t * O : (t + 1) * O], in_=bp1[:, 0:O])
+            nc.scalar.copy(out=bias_t[:, 0:512], in_=bp0[:])
+            nc.scalar.copy(out=bias_t[:, 512:640], in_=bp1[:, 0:O])
 
         g_tiles = {}
         q_tiles = {}
@@ -133,18 +130,11 @@ def tile_skeletonlinear_pa_t_kernel(tc, x, w_self, w_parent, bias, out):
             nc.vector.tensor_copy(
                 out=sv[:], in_=xw[:, :, 0 : VJ * 256].rearrange("p t (w u) -> p t u w", u=2)
             )
-            ss = spool.tile([P, 2, 2, (SJ - VJ) * P], F32, name="ss", tag="ss")
-            nc.scalar.copy(
-                out=ss[:], in_=xw[:, :, VJ * 256 : SJ * 256].rearrange("p t (w u) -> p t u w", u=2)
-            )
-            s_tiles[k] = (sv, ss)
+            s_tiles[k] = sv
 
         def block(k, xw, j, q, u):
-            sv, ss = s_tiles[k]
             if j < VJ:
-                return sv[:, q, u, j * P : (j + 1) * P]
-            if j < SJ:
-                return ss[:, q, u, (j - VJ) * P : (j - VJ + 1) * P]
+                return s_tiles[k][:, q, u, j * P : (j + 1) * P]
             c0 = q * (N * 256) + j * 256
             return xw[:, c0 + u : c0 + 256 : 2]
 
@@ -206,13 +196,13 @@ def tile_skeletonlinear_pa_t_kernel(tc, x, w_self, w_parent, bias, out):
                     mx(dst, xq, xs, (j - 1) * 256 + q * P, 5 + j - 1, True, False)
                 mx(dst, xq, xs, j * 256 + q * P, j, j == 0, True)
             nc.vector.tensor_tensor(
-                out=res[:, t * N * O : t * N * O + 512], in0=acc[:], in1=bias_a[:], op=ADD
+                out=res[:, t * N * O : t * N * O + 512], in0=acc[:], in1=bias_t[:, 0:512], op=ADD
             )
             if t == T - 1:
                 nc.vector.tensor_tensor(
                     out=res[:].rearrange("p (t c) -> p t c", t=T)[:, :, 512:640],
                     in0=acc4[:, 0 : T * O].rearrange("p (t c) -> p t c", t=T),
-                    in1=bias_c[:, 0 : T * O].rearrange("p (t c) -> p t c", t=T),
+                    in1=bias_t[:, 512:640].unsqueeze(1).to_broadcast([P, T, O]),
                     op=ADD,
                 )
                 r0 = chunk_base[c]
@@ -222,14 +212,19 @@ def tile_skeletonlinear_pa_t_kernel(tc, x, w_self, w_parent, bias, out):
 
         weights(0, 5)
         split(0)
+        transposes(0)
+        transposes(1)
+        quantise(0)
+        split(1)
         weights(5, 4)
+        quantise(1)
         spread_bias()
-        for s in range(-LEAD, n_tiles):
-            if s + LEAD + 2 < n_tiles and (s + LEAD) % 2 == 0:
-                split((s + LEAD + 2) // 2)
+        for s in range(2 - LEAD, n_tiles):
             if s + LEAD < n_tiles:
                 transposes(s + LEAD)
-            if 0 <= s + LEAD - 1 < n_tiles:
+            if 2 <= s + LEAD - 1 < n_tiles:
                 quantise(s + LEAD - 1)
             if s >= 0:
                 passes(s)
+            if s + LEAD + 2 < n_tiles and (s + LEAD) % 2 == 0:
+                split((s + LEAD + 2) // 2)

@@ -64,16 +64,16 @@ def tile_skeletonlinear_pa_t_kernel(tc, x, w_self, w_parent, bias, out):
         nc.gpsimd.memset(ones[:], 1.0)
         brow = const.tile([P, 768], BF16, name="brow")
         nc.gpsimd.memset(brow[:], 0.0)
-        wsb = const.tile([P, 9 * I], BF16, name="wsb")
-        nc.sync.dma_start(
-            out=wsb[:, 0 : 5 * I].rearrange("o (n i) -> o n i", n=5),
-            in_=w_self.rearrange("n o i -> o n i"),
-        )
+        w_raw = [const.tile([P, n * I], BF16, name="w_raw%d" % n) for n in (5, 4)]
+
+        def load_weights(kind, w):
+            nc.sync.dma_start(
+                out=w_raw[kind][:].rearrange("o (n i) -> o n i", i=I), in_=w.rearrange("n o i -> o n i")
+            )
+
+        load_weights(0, w_self)
         load(0)
-        nc.sync.dma_start(
-            out=wsb[:, 5 * I : 9 * I].rearrange("o (n i) -> o n i", n=4),
-            in_=w_parent.rearrange("n o i -> o n i"),
-        )
+        load_weights(1, w_parent)
         nc.sync.dma_start(out=brow[0:1, 0 : N * O], in_=bias.unsqueeze(0))
         for k in range(1, XBUFS):
             load(k)
@@ -89,23 +89,23 @@ def tile_skeletonlinear_pa_t_kernel(tc, x, w_self, w_parent, bias, out):
                 in_=tp[:, :, 0 : n * P].rearrange("p u c -> p c u"),
             )
 
-        ww = wsb[:].bitcast(F32)
-        wg = gpool.tile([P, N * 1024], BF16, name="wg", tag="g", align_bytes=64)
-        wg32 = wg[:].bitcast(F32)
-        wq = const.tile([P, 9 * O], U32, name="wq", align_bytes=64)
-        wsc = const.tile([P, 9 * O], U8, name="wsc", align_bytes=64)
+        w_grp = [const.tile([P, n * I], BF16, name="w_grp%d" % n, align_bytes=64) for n in (5, 4)]
+        wq = const.tile([P, 10 * O], U32, name="wq", align_bytes=64)
+        wsc = const.tile([P, 10 * O], U8, name="wsc", align_bytes=64)
 
-        def weights(first, count):
-            for b0 in range(first, first + count, 2):
-                pair = range(b0, min(b0 + 2, first + count))
-                blocks = [[ww[:, b * 256 + u : (b + 1) * 256 : 2] for u in range(2)] for b in pair]
-                flip(blocks, wg32[:, b0 * 256 : (b0 + len(pair)) * 256])
-            for b0, n in ((first, 4), (first + 4, count - 4)):
-                if n:
-                    cols = slice(b0 * O, (b0 + n) * O)
-                    nc.vector.quantize_mx(
-                        out=wq[:, cols].bitcast(FP8X4), scales=wsc[:, cols], in_=wg[:, b0 * I : (b0 + n) * I]
-                    )
+        def weights(kind, count):
+            words = w_raw[kind][:].bitcast(F32)
+            grp = w_grp[kind]
+            for n0 in range(0, count, 2):
+                n1 = min(n0 + 2, count)
+                blocks = [[words[:, n * 256 + u : (n + 1) * 256 : 2] for u in range(2)] for n in range(n0, n1)]
+                flip(blocks, grp[:].bitcast(F32)[:, n0 * 256 : n1 * 256])
+            for n in range(count):
+                b = 2 * n + kind
+                cols = slice(b * O, (b + 1) * O)
+                nc.vector.quantize_mx(
+                    out=wq[:, cols].bitcast(FP8X4), scales=wsc[:, cols], in_=grp[:, n * I : (n + 1) * I]
+                )
 
         bias_t = const.tile([P, N * O], F32, name="bias_t")
 
@@ -168,13 +168,13 @@ def tile_skeletonlinear_pa_t_kernel(tc, x, w_self, w_parent, bias, out):
                     out=xq[:, a:b].bitcast(FP8X4), scales=xs[:, a:b], in_=g[:, 4 * a : 4 * b]
                 )
 
-        def mx(acc, xq, xs, col, b, start, stop):
+        def mx(acc, xq, xs, col, b0, b1, start, stop):
             nc.tensor.matmul_mx(
                 out=acc,
                 lhsT=xq[:, col : col + P].bitcast(FP8X4),
                 lhsT_scale=xs[:, col : col + P],
-                rhs=wq[:, b * O : (b + 1) * O].bitcast(FP8X4),
-                rhs_scale=wsc[:, b * O : (b + 1) * O],
+                rhs=wq[:, b0 * O : b1 * O].bitcast(FP8X4),
+                rhs_scale=wsc[:, b0 * O : b1 * O],
                 start=start,
                 stop=stop,
             )
@@ -190,11 +190,11 @@ def tile_skeletonlinear_pa_t_kernel(tc, x, w_self, w_parent, bias, out):
                 o_tiles[c] = opool.tile([P, T * N * O], F32, name="res", tag="res")
             acc4 = c_tiles[c]
             res = o_tiles[c]
-            for j in range(N):
-                dst = acc[:, j * O : (j + 1) * O] if j < 4 else acc4[:, t * O : (t + 1) * O]
-                if j > 0:
-                    mx(dst, xq, xs, (j - 1) * 256 + q * P, 5 + j - 1, True, False)
-                mx(dst, xq, xs, j * 256 + q * P, j, j == 0, True)
+            for j in (0, 2, 1):
+                mx(acc[:, j * O : (j + 2) * O], xq, xs, j * 256 + q * P, 2 * j, 2 * j + 2, j == 0, False)
+            mx(acc[:, 3 * O : 4 * O], xq, xs, 3 * 256 + q * P, 6, 7, False, True)
+            mx(acc4[:, t * O : (t + 1) * O], xq, xs, 3 * 256 + q * P, 7, 8, True, False)
+            mx(acc4[:, t * O : (t + 1) * O], xq, xs, 4 * 256 + q * P, 8, 9, False, True)
             nc.vector.tensor_tensor(
                 out=res[:, t * N * O : t * N * O + 512], in0=acc[:], in1=bias_t[:, 0:512], op=ADD
             )
@@ -216,7 +216,7 @@ def tile_skeletonlinear_pa_t_kernel(tc, x, w_self, w_parent, bias, out):
         transposes(1)
         quantise(0)
         split(1)
-        weights(5, 4)
+        weights(1, 4)
         quantise(1)
         spread_bias()
         for s in range(2 - LEAD, n_tiles):

@@ -18,7 +18,7 @@ CHUNKS = [4, 4, 4, 4, 4, 4, 4, 2, 2]
 XBUFS = 9
 OBUFS = 4
 LEAD = 3
-VJ = 2
+SPLIT = (2, 4)
 
 
 def tile_skeletonlinear_pa_t_kernel(tc, x, w_self, w_parent, bias, out):
@@ -78,13 +78,13 @@ def tile_skeletonlinear_pa_t_kernel(tc, x, w_self, w_parent, bias, out):
         for k in range(1, XBUFS):
             load(k)
 
-        def flip(blocks, dst32):
+        def flip(blocks, dst32, copy=nc.scalar.copy):
             n = len(blocks)
             tp = pst.tile([P, 2, 256], F32, name="tp", tag="tp")
             for u in range(2):
                 for q in range(n):
                     nc.tensor.transpose(tp[:, u, q * P : (q + 1) * P], blocks[q][u], ident[:])
-            nc.scalar.copy(
+            copy(
                 out=dst32.rearrange("p (c u) -> p c u", u=2),
                 in_=tp[:, :, 0 : n * P].rearrange("p u c -> p c u"),
             )
@@ -126,15 +126,17 @@ def tile_skeletonlinear_pa_t_kernel(tc, x, w_self, w_parent, bias, out):
 
         def split(k):
             xw = x_tiles[k][:].bitcast(F32).rearrange("p (t w) -> p t w", t=2)
-            sv = spool.tile([P, 2, 2, VJ * P], F32, name="sv", tag="sv")
+            j0, j1 = SPLIT
+            sv = spool.tile([P, 2, 2, (j1 - j0) * P], F32, name="sv", tag="sv")
             nc.vector.tensor_copy(
-                out=sv[:], in_=xw[:, :, 0 : VJ * 256].rearrange("p t (w u) -> p t u w", u=2)
+                out=sv[:], in_=xw[:, :, j0 * 256 : j1 * 256].rearrange("p t (w u) -> p t u w", u=2)
             )
             s_tiles[k] = sv
 
         def block(k, xw, j, q, u):
-            if j < VJ:
-                return s_tiles[k][:, q, u, j * P : (j + 1) * P]
+            j0, j1 = SPLIT
+            if j0 <= j < j1:
+                return s_tiles[k][:, q, u, (j - j0) * P : (j - j0 + 1) * P]
             c0 = q * (N * 256) + j * 256
             return xw[:, c0 + u : c0 + 256 : 2]
 
@@ -148,6 +150,7 @@ def tile_skeletonlinear_pa_t_kernel(tc, x, w_self, w_parent, bias, out):
                 flip(
                     [[block(k, xw, j, q, u) for u in range(2)] for q in range(2)],
                     g32[:, j * 512 : (j + 1) * 512],
+                    nc.vector.tensor_copy if k == 0 and j in (1, 3) else nc.scalar.copy,
                 )
             if part == 1 and k + XBUFS < n_tiles // 2:
                 load(k + XBUFS)

@@ -18,7 +18,8 @@ CHUNKS = [4, 4, 4, 4, 4, 4, 4, 2, 2]
 XBUFS = 9
 OBUFS = 4
 LEAD = 3
-SPLIT = (2, 4)
+V_SPLIT = (0, 2, 5)
+S_SPLIT = (1, 4, 5)
 
 
 def tile_skeletonlinear_pa_t_kernel(tc, x, w_self, w_parent, bias, out):
@@ -124,19 +125,23 @@ def tile_skeletonlinear_pa_t_kernel(tc, x, w_self, w_parent, bias, out):
 
         s_tiles = {}
 
-        def split(k):
+        def split(k, part, copy, name):
+            q, j0, j1 = part
             xw = x_tiles[k][:].bitcast(F32).rearrange("p (t w) -> p t w", t=2)
-            j0, j1 = SPLIT
-            sv = spool.tile([P, 2, 2, (j1 - j0) * P], F32, name="sv", tag="sv")
-            nc.vector.tensor_copy(
-                out=sv[:], in_=xw[:, :, j0 * 256 : j1 * 256].rearrange("p t (w u) -> p t u w", u=2)
-            )
-            s_tiles[k] = sv
+            sp = spool.tile([P, 2, (j1 - j0) * P], F32, name=name, tag=name)
+            copy(out=sp[:], in_=xw[:, q, j0 * 256 : j1 * 256].rearrange("p (w u) -> p u w", u=2))
+            for j in range(j0, j1):
+                s_tiles[k, j, q] = sp[:, :, (j - j0) * P : (j - j0 + 1) * P]
+
+        def split_v(k):
+            split(k, V_SPLIT, nc.vector.tensor_copy, "sv")
+
+        def split_s(k):
+            split(k, S_SPLIT, nc.scalar.copy, "ss")
 
         def block(k, xw, j, q, u):
-            j0, j1 = SPLIT
-            if j0 <= j < j1:
-                return s_tiles[k][:, q, u, (j - j0) * P : (j - j0 + 1) * P]
+            if (k, j, q) in s_tiles:
+                return s_tiles[k, j, q][:, u, :]
             c0 = q * (N * 256) + j * 256
             return xw[:, c0 + u : c0 + 256 : 2]
 
@@ -214,11 +219,11 @@ def tile_skeletonlinear_pa_t_kernel(tc, x, w_self, w_parent, bias, out):
                 )
 
         weights(0, 5)
-        split(0)
+        split_v(0)
         transposes(0)
         transposes(1)
         quantise(0)
-        split(1)
+        split_v(1)
         weights(1, 4)
         quantise(1)
         spread_bias()
@@ -230,4 +235,6 @@ def tile_skeletonlinear_pa_t_kernel(tc, x, w_self, w_parent, bias, out):
             if s >= 0:
                 passes(s)
             if s + LEAD + 2 < n_tiles and (s + LEAD) % 2 == 0:
-                split((s + LEAD + 2) // 2)
+                split_v((s + LEAD + 2) // 2)
+            if s + LEAD + 1 < n_tiles and (s + LEAD) % 2 == 1:
+                split_s((s + LEAD + 1) // 2)

@@ -17,7 +17,6 @@ FLOPS = 2 * B * I * O * (2 * N - 1)
 CHUNKS = [4, 4, 4, 4, 4, 4, 4, 2, 2]
 XBUFS = 9
 OBUFS = 4
-LEAD = 3
 V_SPLIT = (0, 2, 5)
 S_SPLIT = (1, 4, 5)
 
@@ -32,7 +31,7 @@ def tile_skeletonlinear_pa_t_kernel(tc, x, w_self, w_parent, bias, out):
         chunk_base.append(P * len(tiles))
         for t in range(T):
             tiles.append((c, t))
-    n_tiles = len(tiles)
+    n_pairs = len(tiles) // 2
 
     with ExitStack() as ctx:
         const = ctx.enter_context(tc.tile_pool(name="const", bufs=1))
@@ -41,9 +40,9 @@ def tile_skeletonlinear_pa_t_kernel(tc, x, w_self, w_parent, bias, out):
         qpool = ctx.enter_context(tc.tile_pool(name="qnt", bufs=4))
         spool = ctx.enter_context(tc.tile_pool(name="spl", bufs=2))
         opool = ctx.enter_context(tc.tile_pool(name="res", bufs=OBUFS))
-        pst = ctx.enter_context(tc.psum_pool(name="pst", bufs=4))
+        pst = ctx.enter_context(tc.psum_pool(name="pst", bufs=5))
         pso = ctx.enter_context(tc.psum_pool(name="pso", bufs=2))
-        psc = ctx.enter_context(tc.psum_pool(name="psc", bufs=2))
+        psc = ctx.enter_context(tc.psum_pool(name="psc", bufs=1))
         ctx.enter_context(tc.manual_schedule())
 
         x_tiles = {}
@@ -145,33 +144,25 @@ def tile_skeletonlinear_pa_t_kernel(tc, x, w_self, w_parent, bias, out):
             c0 = q * (N * 256) + j * 256
             return xw[:, c0 + u : c0 + 256 : 2]
 
-        def transposes(h):
-            k, part = divmod(h, 2)
+        def transposes(k):
             xw = x_tiles[k][:].bitcast(F32)
-            if part == 0:
-                g_tiles[k] = gpool.tile([P, N * 1024], BF16, name="g", tag="g", align_bytes=64)
+            g_tiles[k] = gpool.tile([P, N * 1024], BF16, name="g", tag="g", align_bytes=64)
             g32 = g_tiles[k][:].bitcast(F32)
-            for j in ((0, 1) if part == 0 else (2, 3, 4)):
+            for j in range(N):
                 flip(
                     [[block(k, xw, j, q, u) for u in range(2)] for q in range(2)],
                     g32[:, j * 512 : (j + 1) * 512],
                     nc.vector.tensor_copy if k == 0 and j in (1, 3) else nc.scalar.copy,
                 )
-            if part == 1 and k + XBUFS < n_tiles // 2:
+            if k + XBUFS < n_pairs:
                 load(k + XBUFS)
 
-        def quantise(h):
-            k, part = divmod(h, 2)
+        def quantise(k):
             g = g_tiles[k]
-            if part == 0:
-                xq = qpool.tile([P, N * 256], U32, name="xq", tag="xq", align_bytes=64)
-                xs = qpool.tile([P, N * 256], U8, name="xs", tag="xs", align_bytes=64)
-                q_tiles[k] = (xq, xs)
-                spans = [(0, 512)]
-            else:
-                xq, xs = q_tiles[k]
-                spans = [(512, 1024), (1024, 1280)]
-            for a, b in spans:
+            xq = qpool.tile([P, N * 256], U32, name="xq", tag="xq", align_bytes=64)
+            xs = qpool.tile([P, N * 256], U8, name="xs", tag="xs", align_bytes=64)
+            q_tiles[k] = (xq, xs)
+            for a, b in ((0, 1024), (1024, 1280)):
                 nc.vector.quantize_mx(
                     out=xq[:, a:b].bitcast(FP8X4), scales=xs[:, a:b], in_=g[:, 4 * a : 4 * b]
                 )
@@ -206,14 +197,25 @@ def tile_skeletonlinear_pa_t_kernel(tc, x, w_self, w_parent, bias, out):
             nc.vector.tensor_tensor(
                 out=res[:, t * N * O : t * N * O + 512], in0=acc[:], in1=bias_t[:, 0:512], op=ADD
             )
-            if t == T - 1:
+            r0 = chunk_base[c]
+            if c == len(CHUNKS) - 1:
+                nc.vector.tensor_tensor(
+                    out=res[:, t * N * O + 512 : (t + 1) * N * O],
+                    in0=acc4[:, t * O : (t + 1) * O],
+                    in1=bias_t[:, 512:640],
+                    op=ADD,
+                )
+                nc.sync.dma_start(
+                    out=out[r0 : r0 + P * T, :].rearrange("(p t) c -> p t c", t=T)[:, t, :],
+                    in_=res[:, t * N * O : (t + 1) * N * O],
+                )
+            elif t == T - 1:
                 nc.vector.tensor_tensor(
                     out=res[:].rearrange("p (t c) -> p t c", t=T)[:, :, 512:640],
                     in0=acc4[:, 0 : T * O].rearrange("p (t c) -> p t c", t=T),
                     in1=bias_t[:, 512:640].unsqueeze(1).to_broadcast([P, T, O]),
                     op=ADD,
                 )
-                r0 = chunk_base[c]
                 nc.sync.dma_start(
                     out=out[r0 : r0 + P * T, :].rearrange("(p t) c -> p (t c)", t=T), in_=res[:]
                 )
@@ -221,20 +223,18 @@ def tile_skeletonlinear_pa_t_kernel(tc, x, w_self, w_parent, bias, out):
         weights(0, 5)
         split_v(0)
         transposes(0)
-        transposes(1)
-        quantise(0)
         split_v(1)
         weights(1, 4)
-        quantise(1)
         spread_bias()
-        for s in range(2 - LEAD, n_tiles):
-            if s + LEAD < n_tiles:
-                transposes(s + LEAD)
-            if 2 <= s + LEAD - 1 < n_tiles:
-                quantise(s + LEAD - 1)
-            if s >= 0:
-                passes(s)
-            if s + LEAD + 2 < n_tiles and (s + LEAD) % 2 == 0:
-                split_v((s + LEAD + 2) // 2)
-            if s + LEAD + 1 < n_tiles and (s + LEAD) % 2 == 1:
-                split_s((s + LEAD + 1) // 2)
+        for k in range(-1, n_pairs):
+            if k + 2 < n_pairs:
+                transposes(k + 2)
+            if 2 <= k + 3 < n_pairs:
+                split_s(k + 3)
+            if k + 1 < n_pairs:
+                quantise(k + 1)
+            if k + 3 < n_pairs:
+                split_v(k + 3)
+            if k >= 0:
+                passes(2 * k)
+                passes(2 * k + 1)

@@ -50,7 +50,7 @@ def tile_skeletonlinear_pa_t_kernel(tc, x, w_self, w_parent, bias, out):
         def load(k):
             c, t0 = tiles[2 * k]
             T = CHUNKS[c]
-            xt = xpool.tile([P, 2 * N * I], BF16, name="xt", tag="xt")
+            xt = xpool.tile([P, 2 * N * I], BF16, name="xt", tag="xt", align_bytes=256)
             r0 = chunk_base[c]
             rows = x[r0 : r0 + P * T, :].rearrange("(p t) c -> p t c", t=T)
             nc.sync.dma_start(
@@ -64,26 +64,32 @@ def tile_skeletonlinear_pa_t_kernel(tc, x, w_self, w_parent, bias, out):
         nc.gpsimd.memset(ones[:], 1.0)
         brow = const.tile([P, 768], BF16, name="brow")
         nc.gpsimd.memset(brow[:], 0.0)
-        w_raw = [const.tile([P, n * I], BF16, name="w_raw%d" % n) for n in (5, 4)]
+        w_raw = [const.tile([P, n * I], BF16, name="w_raw%d" % n, align_bytes=256) for n in (5, 4)]
 
         def load_weights(kind, w):
             nc.sync.dma_start(
-                out=w_raw[kind][:].rearrange("o (n i) -> o n i", i=I), in_=w.rearrange("n o i -> o n i")
+                out=w_raw[kind][:, 0 : 4 * I],
+                in_=w[0:4].rearrange("n o i -> (n o) i").rearrange("(p r) i -> p (r i)", r=4),
             )
 
         load_weights(0, w_self)
+        nc.sync.dma_start(out=w_raw[0][:, 4 * I : 5 * I], in_=w_self[4])
         load(0)
         load_weights(1, w_parent)
         nc.sync.dma_start(out=brow[0:1, 0 : N * O], in_=bias.unsqueeze(0))
         for k in range(1, XBUFS):
             load(k)
 
-        def flip(blocks, dst32, copy=nc.scalar.copy):
-            n = len(blocks)
+        def turn(blocks):
             tp = pst.tile([P, 2, 256], F32, name="tp", tag="tp")
             for u in range(2):
-                for q in range(n):
+                for q in range(len(blocks)):
                     nc.tensor.transpose(tp[:, u, q * P : (q + 1) * P], blocks[q][u], ident[:])
+            return tp
+
+        def flip(blocks, dst32, copy=nc.scalar.copy):
+            tp = turn(blocks)
+            n = len(blocks)
             copy(
                 out=dst32.rearrange("p (c u) -> p c u", u=2),
                 in_=tp[:, :, 0 : n * P].rearrange("p u c -> p c u"),
@@ -95,16 +101,30 @@ def tile_skeletonlinear_pa_t_kernel(tc, x, w_self, w_parent, bias, out):
 
         def weights(kind, count):
             words = w_raw[kind][:].bitcast(F32)
-            grp = w_grp[kind]
-            for n0 in range(0, count, 2):
-                n1 = min(n0 + 2, count)
-                blocks = [[words[:, n * 256 + u : (n + 1) * 256 : 2] for u in range(2)] for n in range(n0, n1)]
-                flip(blocks, grp[:].bitcast(F32)[:, n0 * 256 : n1 * 256])
+            grp32 = w_grp[kind][:].bitcast(F32)
+
+            def block(b):
+                return [words[:, b * 256 + u : (b + 1) * 256 : 2] for u in range(2)]
+
+            grp = grp32[:, 0:1024].rearrange("k (n r m u) -> k r n m u", n=4, r=4, u=2)
+            for r in (0, 2):
+                tp = turn([block(r), block(r + 1)])
+                for q in range(2):
+                    nc.scalar.copy(
+                        out=grp[:, r + q],
+                        in_=tp[:, :, q * P : (q + 1) * P].rearrange("k u (n m) -> k n m u", n=4),
+                    )
+            if count == 5:
+                tp = turn([block(4)])
+                nc.scalar.copy(
+                    out=grp32[:, 1024:1280].rearrange("k (r m u) -> k r m u", r=4, u=2),
+                    in_=tp[:, :, 0:P].rearrange("k u (m r) -> k r m u", r=4),
+                )
             for n in range(count):
                 b = 2 * n + kind
                 cols = slice(b * O, (b + 1) * O)
                 nc.vector.quantize_mx(
-                    out=wq[:, cols].bitcast(FP8X4), scales=wsc[:, cols], in_=grp[:, n * I : (n + 1) * I]
+                    out=wq[:, cols].bitcast(FP8X4), scales=wsc[:, cols], in_=w_grp[kind][:, n * I : (n + 1) * I]
                 )
 
         bias_t = const.tile([P, N * O], F32, name="bias_t")
@@ -186,7 +206,7 @@ def tile_skeletonlinear_pa_t_kernel(tc, x, w_self, w_parent, bias, out):
             acc = pso.tile([P, 512], F32, name="acc", tag="o")
             if t == 0:
                 c_tiles[c] = psc.tile([P, 512], F32, name="acc4", tag="c")
-                o_tiles[c] = opool.tile([P, T * N * O], F32, name="res", tag="res")
+                o_tiles[c] = opool.tile([P, T * N * O], F32, name="res", tag="res", align_bytes=256)
             acc4 = c_tiles[c]
             res = o_tiles[c]
             for j in (0, 2, 1):
@@ -194,26 +214,27 @@ def tile_skeletonlinear_pa_t_kernel(tc, x, w_self, w_parent, bias, out):
             mx(acc[:, 3 * O : 4 * O], xq, xs, 3 * 256 + q * P, 6, 7, False, True)
             mx(acc4[:, t * O : (t + 1) * O], xq, xs, 3 * 256 + q * P, 7, 8, True, False)
             mx(acc4[:, t * O : (t + 1) * O], xq, xs, 4 * 256 + q * P, 8, 9, False, True)
+            row = res[:].rearrange("p (t n m r) -> p t n m r", t=T, n=N, r=4)
+            b4 = bias_t[:].rearrange("p (n m r) -> p n m r", n=N, r=4)
             nc.vector.tensor_tensor(
-                out=res[:, t * N * O : t * N * O + 512], in0=acc[:], in1=bias_t[:, 0:512], op=ADD
+                out=row[:, t, 0:4],
+                in0=acc[:].rearrange("p (n r m) -> p n m r", n=4, r=4),
+                in1=b4[:, 0:4],
+                op=ADD,
             )
+            last = acc4[:].rearrange("p (t r m) -> p t m r", t=4, r=4)
             r0 = chunk_base[c]
             if c == len(CHUNKS) - 1:
-                nc.vector.tensor_tensor(
-                    out=res[:, t * N * O + 512 : (t + 1) * N * O],
-                    in0=acc4[:, t * O : (t + 1) * O],
-                    in1=bias_t[:, 512:640],
-                    op=ADD,
-                )
+                nc.vector.tensor_tensor(out=row[:, t, 4], in0=last[:, t], in1=b4[:, 4], op=ADD)
                 nc.sync.dma_start(
                     out=out[r0 : r0 + P * T, :].rearrange("(p t) c -> p t c", t=T)[:, t, :],
                     in_=res[:, t * N * O : (t + 1) * N * O],
                 )
             elif t == T - 1:
                 nc.vector.tensor_tensor(
-                    out=res[:].rearrange("p (t c) -> p t c", t=T)[:, :, 512:640],
-                    in0=acc4[:, 0 : T * O].rearrange("p (t c) -> p t c", t=T),
-                    in1=bias_t[:, 512:640].unsqueeze(1).to_broadcast([P, T, O]),
+                    out=row[:, :, 4],
+                    in0=last[:, 0:T],
+                    in1=b4[:, 4].unsqueeze(1).to_broadcast([P, T, 32, 4]),
                     op=ADD,
                 )
                 nc.sync.dma_start(

from contextlib import ExitStack

import concourse.mybir as mybir
from concourse.masks import make_identity

F32 = mybir.dt.float32
BF16 = mybir.dt.bfloat16
U32 = mybir.dt.uint32
U8 = mybir.dt.uint8
FP8X4 = mybir.dt.float8_e4m3fn_x4
ADD = mybir.AluOpType.add

P = 128
B, N, I, O = 4096, 5, 512, 128
FLOPS = 2 * B * I * O * (2 * N - 1)

CHUNKS = [4, 4, 4, 4, 4, 4, 4, 2, 2]
XBUFS = 9
OBUFS = 4
V_SPLIT = (0, 2, 5)
S_SPLIT = (1, 4, 5)


def tile_skeletonlinear_pa_t_kernel(tc, x, w_self, w_parent, bias, out):
    nc = tc.nc
    assert sum(CHUNKS) * P == B

    chunk_base = []
    tiles = []
    for c, T in enumerate(CHUNKS):
        chunk_base.append(P * len(tiles))
        for t in range(T):
            tiles.append((c, t))
    n_pairs = len(tiles) // 2

    with ExitStack() as ctx:
        const = ctx.enter_context(tc.tile_pool(name="const", bufs=1))
        xpool = ctx.enter_context(tc.tile_pool(name="xin", bufs=XBUFS))
        gpool = ctx.enter_context(tc.tile_pool(name="grp", bufs=3))
        qpool = ctx.enter_context(tc.tile_pool(name="qnt", bufs=4))
        spool = ctx.enter_context(tc.tile_pool(name="spl", bufs=2))
        opool = ctx.enter_context(tc.tile_pool(name="res", bufs=OBUFS))
        pst = ctx.enter_context(tc.psum_pool(name="pst", bufs=5))
        pso = ctx.enter_context(tc.psum_pool(name="pso", bufs=2))
        psc = ctx.enter_context(tc.psum_pool(name="psc", bufs=1))
        ctx.enter_context(tc.manual_schedule())

        x_tiles = {}

        def load(k):
            c, t0 = tiles[2 * k]
            T = CHUNKS[c]
            xt = xpool.tile([P, 2 * N * I], BF16, name="xt", tag="xt", align_bytes=256)
            r0 = chunk_base[c]
            rows = x[r0 : r0 + P * T, :].rearrange("(p t) c -> p t c", t=T)
            nc.sync.dma_start(
                out=xt[:].rearrange("p (t c) -> p t c", t=2), in_=rows[:, t0 : t0 + 2, :]
            )
            x_tiles[k] = xt

        ident = const.tile([P, P], F32, name="ident")
        make_identity(nc, ident[:])
        ones = const.tile([P, P], BF16, name="ones")
        nc.gpsimd.memset(ones[:], 1.0)
        brow = const.tile([P, 768], BF16, name="brow")
        nc.gpsimd.memset(brow[:], 0.0)
        w_raw = [const.tile([P, n * I], BF16, name="w_raw%d" % n, align_bytes=256) for n in (5, 4)]

        def load_weights(kind, w):
            nc.sync.dma_start(
                out=w_raw[kind][:, 0 : 4 * I],
                in_=w[0:4].rearrange("n o i -> (n o) i").rearrange("(p r) i -> p (r i)", r=4),
            )

        load_weights(0, w_self)
        nc.sync.dma_start(out=w_raw[0][:, 4 * I : 5 * I], in_=w_self[4])
        load(0)
        load_weights(1, w_parent)
        nc.sync.dma_start(out=brow[0:1, 0 : N * O], in_=bias.unsqueeze(0))
        for k in range(1, XBUFS):
            load(k)

        def turn(blocks):
            tp = pst.tile([P, 2, 256], F32, name="tp", tag="tp")
            for u in range(2):
                for q in range(len(blocks)):
                    nc.tensor.transpose(tp[:, u, q * P : (q + 1) * P], blocks[q][u], ident[:])
            return tp

        def flip(blocks, dst32, copy=nc.scalar.copy):
            tp = turn(blocks)
            n = len(blocks)
            copy(
                out=dst32.rearrange("p (c u) -> p c u", u=2),
                in_=tp[:, :, 0 : n * P].rearrange("p u c -> p c u"),
            )

        w_grp = [const.tile([P, n * I], BF16, name="w_grp%d" % n, align_bytes=64) for n in (5, 4)]
        wq = const.tile([P, 10 * O], U32, name="wq", align_bytes=64)
        wsc = const.tile([P, 10 * O], U8, name="wsc", align_bytes=64)

        def weights(kind, count):
            words = w_raw[kind][:].bitcast(F32)
            grp32 = w_grp[kind][:].bitcast(F32)

            def block(b):
                return [words[:, b * 256 + u : (b + 1) * 256 : 2] for u in range(2)]

            grp = grp32[:, 0:1024].rearrange("k (n r m u) -> k r n m u", n=4, r=4, u=2)
            for r in (0, 2):
                tp = turn([block(r), block(r + 1)])
                for q in range(2):
                    nc.scalar.copy(
                        out=grp[:, r + q],
                        in_=tp[:, :, q * P : (q + 1) * P].rearrange("k u (n m) -> k n m u", n=4),
                    )
            if count == 5:
                tp = turn([block(4)])
                nc.scalar.copy(
                    out=grp32[:, 1024:1280].rearrange("k (r m u) -> k r m u", r=4, u=2),
                    in_=tp[:, :, 0:P].rearrange("k u (m r) -> k r m u", r=4),
                )
            for n in range(count):
                b = 2 * n + kind
                cols = slice(b * O, (b + 1) * O)
                nc.vector.quantize_mx(
                    out=wq[:, cols].bitcast(FP8X4), scales=wsc[:, cols], in_=w_grp[kind][:, n * I : (n + 1) * I]
                )

        bias_t = const.tile([P, N * O], F32, name="bias_t")

        def spread_bias():
            bp0 = pso.tile([P, 512], F32, name="bp0", tag="o")
            nc.tensor.matmul(bp0[:], lhsT=ones[:], rhs=brow[:, 0:512], start=True, stop=True)
            bp1 = pso.tile([P, 512], F32, name="bp1", tag="o")
            nc.tensor.matmul(bp1[:, 0:256], lhsT=ones[:], rhs=brow[:, 512:768], start=True, stop=True)
            nc.scalar.copy(out=bias_t[:, 0:512], in_=bp0[:])
            nc.scalar.copy(out=bias_t[:, 512:640], in_=bp1[:, 0:O])

        g_tiles = {}
        q_tiles = {}
        c_tiles = {}
        o_tiles = {}

        s_tiles = {}

        def split(k, part, copy, name):
            q, j0, j1 = part
            xw = x_tiles[k][:].bitcast(F32).rearrange("p (t w) -> p t w", t=2)
            sp = spool.tile([P, 2, (j1 - j0) * P], F32, name=name, tag=name)
            copy(out=sp[:], in_=xw[:, q, j0 * 256 : j1 * 256].rearrange("p (w u) -> p u w", u=2))
            for j in range(j0, j1):
                s_tiles[k, j, q] = sp[:, :, (j - j0) * P : (j - j0 + 1) * P]

        def split_v(k):
            split(k, V_SPLIT, nc.vector.tensor_copy, "sv")

        def split_s(k):
            split(k, S_SPLIT, nc.scalar.copy, "ss")

        def block(k, xw, j, q, u):
            if (k, j, q) in s_tiles:
                return s_tiles[k, j, q][:, u, :]
            c0 = q * (N * 256) + j * 256
            return xw[:, c0 + u : c0 + 256 : 2]

        def transposes(k):
            xw = x_tiles[k][:].bitcast(F32)
            g_tiles[k] = gpool.tile([P, N * 1024], BF16, name="g", tag="g", align_bytes=64)
            g32 = g_tiles[k][:].bitcast(F32)
            for j in range(N):
                flip(
                    [[block(k, xw, j, q, u) for u in range(2)] for q in range(2)],
                    g32[:, j * 512 : (j + 1) * 512],
                    nc.vector.tensor_copy if k == 0 and j in (1, 3) else nc.scalar.copy,
                )
            if k + XBUFS < n_pairs:
                load(k + XBUFS)

        def quantise(k):
            g = g_tiles[k]
            xq = qpool.tile([P, N * 256], U32, name="xq", tag="xq", align_bytes=64)
            xs = qpool.tile([P, N * 256], U8, name="xs", tag="xs", align_bytes=64)
            q_tiles[k] = (xq, xs)
            for a, b in ((0, 1024), (1024, 1280)):
                nc.vector.quantize_mx(
                    out=xq[:, a:b].bitcast(FP8X4), scales=xs[:, a:b], in_=g[:, 4 * a : 4 * b]
                )

        def mx(acc, xq, xs, col, b0, b1, start, stop):
            nc.tensor.matmul_mx(
                out=acc,
                lhsT=xq[:, col : col + P].bitcast(FP8X4),
                lhsT_scale=xs[:, col : col + P],
                rhs=wq[:, b0 * O : b1 * O].bitcast(FP8X4),
                rhs_scale=wsc[:, b0 * O : b1 * O],
                start=start,
                stop=stop,
            )

        def passes(s):
            c, t = tiles[s]
            T = CHUNKS[c]
            xq, xs = q_tiles[s // 2]
            q = s % 2
            acc = pso.tile([P, 512], F32, name="acc", tag="o")
            if t == 0:
                c_tiles[c] = psc.tile([P, 512], F32, name="acc4", tag="c")
                o_tiles[c] = opool.tile([P, T * N * O], F32, name="res", tag="res", align_bytes=256)
            acc4 = c_tiles[c]
            res = o_tiles[c]
            for j in (0, 2, 1):
                mx(acc[:, j * O : (j + 2) * O], xq, xs, j * 256 + q * P, 2 * j, 2 * j + 2, j == 0, False)
            mx(acc[:, 3 * O : 4 * O], xq, xs, 3 * 256 + q * P, 6, 7, False, True)
            mx(acc4[:, t * O : (t + 1) * O], xq, xs, 3 * 256 + q * P, 7, 8, True, False)
            mx(acc4[:, t * O : (t + 1) * O], xq, xs, 4 * 256 + q * P, 8, 9, False, True)
            row = res[:].rearrange("p (t n m r) -> p t n m r", t=T, n=N, r=4)
            b4 = bias_t[:].rearrange("p (n m r) -> p n m r", n=N, r=4)
            nc.vector.tensor_tensor(
                out=row[:, t, 0:4],
                in0=acc[:].rearrange("p (n r m) -> p n m r", n=4, r=4),
                in1=b4[:, 0:4],
                op=ADD,
            )
            last = acc4[:].rearrange("p (t r m) -> p t m r", t=4, r=4)
            r0 = chunk_base[c]
            if c == len(CHUNKS) - 1:
                nc.vector.tensor_tensor(out=row[:, t, 4], in0=last[:, t], in1=b4[:, 4], op=ADD)
                nc.sync.dma_start(
                    out=out[r0 : r0 + P * T, :].rearrange("(p t) c -> p t c", t=T)[:, t, :],
                    in_=res[:, t * N * O : (t + 1) * N * O],
                )
            elif t == T - 1:
                nc.vector.tensor_tensor(
                    out=row[:, :, 4],
                    in0=last[:, 0:T],
                    in1=b4[:, 4].unsqueeze(1).to_broadcast([P, T, 32, 4]),
                    op=ADD,
                )
                nc.sync.dma_start(
                    out=out[r0 : r0 + P * T, :].rearrange("(p t) c -> p (t c)", t=T), in_=res[:]
                )

        weights(0, 5)
        split_v(0)
        transposes(0)
        split_v(1)
        weights(1, 4)
        spread_bias()
        for k in range(-1, n_pairs):
            if k + 2 < n_pairs:
                transposes(k + 2)
            if 2 <= k + 3 < n_pairs:
                split_s(k + 3)
            if k + 1 < n_pairs:
                quantise(k + 1)
            if k + 3 < n_pairs:
                split_v(k + 3)
            if k >= 0:
                passes(2 * k)
                passes(2 * k + 1)
